import numpy as np
import ml_dtypes


def mxq(x, axis, fmt="e4m3"):
    dtype, down = {"e4m3": (ml_dtypes.float8_e4m3fn, 7), "e5m2": (ml_dtypes.float8_e5m2, 14)}[fmt]
    v = np.moveaxis(np.asarray(x, np.float32).astype(ml_dtypes.bfloat16).astype(np.float64), axis, -1)
    blocks = v.reshape(v.shape[:-1] + (-1, 32))
    amax = np.abs(blocks).max(-1, keepdims=True)
    byte = np.maximum(np.where(amax > 0, np.frexp(amax)[1] - 1 + 127, 0) - down, 1)
    scale = np.exp2(byte - 127.0)
    codes = (blocks / scale).astype(np.float32).astype(dtype).astype(np.float64)
    return np.moveaxis((codes * scale).reshape(v.shape), -1, axis)


WIDE = False


def mx_kscale(k):
    if not WIDE:
        return np.ones(k)
    levels = np.array([10, -10, 5, -5, 0])
    a = np.random.permutation(np.resize(levels, k // 512 * 4)).reshape(k // 512, 4)
    idx = np.arange(k)
    return np.exp2(a[idx // 512, idx % 128 // 32])


BF16 = ml_dtypes.bfloat16


def bf(x):
    return np.asarray(x, np.float32).astype(BF16)


def f64(x):
    return np.asarray(x).astype(np.float64)


B, T, E, V, NH, C = 1, 256, 512, 2048, 4, 512
KD = E // NH
SCALING = KD ** -0.5


def rotate_every_two(x):
    x1 = x[..., 0::2]
    x2 = x[..., 1::2]
    return np.stack((-x2, x1), axis=-1).reshape(x.shape)


def theta_shift(x, sin, cos):
    return x * cos + rotate_every_two(x) * sin


def rope_tables():
    half = np.arange(0, KD, 2) / KD
    angle = np.repeat(1.0 / 10000.0 ** half, 2)
    pos = np.arange(T)
    return np.sin(pos[:, None] * angle[None, :]), np.cos(pos[:, None] * angle[None, :])


def setup_inputs():
    s = mx_kscale(E)
    sin, cos = rope_tables()
    return {"hidden_states": bf(np.random.standard_normal((B, T, E)) * s),
            "wq": bf(np.random.standard_normal((E, E)) / np.sqrt(E) / s[None, :]),
            "wk": bf(np.random.standard_normal((E, E)) * 2.0 / np.sqrt(E) / s[None, :]),
            "sin": bf(sin), "cos": bf(cos)}


def reference(hidden_states, wq, wk, sin, cos):
    xq = mxq(f64(hidden_states), 2, "e4m3")
    q = xq @ mxq(f64(wq), 1, "e4m3").T
    k = xq @ mxq(f64(wk), 1, "e4m3").T
    q = q.reshape(B, T, NH, KD).transpose(0, 2, 1, 3)
    k = k.reshape(B, T, NH, KD).transpose(0, 2, 1, 3) * SCALING
    return theta_shift(q, f64(sin), f64(cos)), theta_shift(k, f64(sin), f64(cos))

@@ -1,0 +1,134 @@
+from contextlib import ExitStack
+
+import concourse.mybir as mybir
+from concourse.masks import make_identity
+
+BF16 = mybir.dt.bfloat16
+F32 = mybir.dt.float32
+U32 = mybir.dt.uint32
+U8 = mybir.dt.uint8
+FP8X4 = mybir.dt.float8_e4m3fn_x4
+MULT = mybir.AluOpType.mult
+ADD = mybir.AluOpType.add
+
+P = 128
+T = 256
+E = 512
+HEADS = 4
+HEAD_DIM = 128
+PAIRS = HEAD_DIM // 2
+SCALING = HEAD_DIM**-0.5
+WORDS = E // 2
+SLAB = 2 * P
+FLOPS = 2 * T * E * (2 * E)
+
+
+def tile_nucleusxmultiscaleretention_pa_s_kernel(
+    tc, hidden_states, wq, wk, sin, cos, out_0, out_1
+):
+    nc = tc.nc
+    with ExitStack() as ctx:
+        keep = ctx.enter_context(tc.tile_pool(name="keep", bufs=1))
+        stage = ctx.enter_context(tc.tile_pool(name="stage", bufs=3))
+        rotated = ctx.enter_context(tc.tile_pool(name="rotated", bufs=4))
+        flip_banks = ctx.enter_context(tc.psum_pool(name="flip_banks", bufs=4))
+        product_banks = ctx.enter_context(tc.psum_pool(name="product_banks", bufs=2))
+
+        x_rows = hidden_states.flatten_outer_dims().rearrange("(p j) k -> p j k", j=2)
+        wq_rows = wq.rearrange("(j p c) k -> c p j k", j=2, c=2)
+        wk_rows = wk.rearrange("(j p c) k -> c p j k", j=2, c=2)
+
+        def load_slab(label, rows):
+            raw = keep.tile([P, 2 * E], BF16, name="raw_" + label)
+            nc.sync.dma_start(out=raw[:].rearrange("p (j k) -> p j k", j=2), in_=rows)
+            return raw
+
+        cos_sb = keep.tile([P, 2 * HEAD_DIM], BF16)
+        sin_sb = keep.tile([P, 2 * HEAD_DIM], BF16)
+        nc.scalar.dma_start(out=cos_sb[:], in_=cos.rearrange("(p j) d -> p (j d)", j=2))
+        nc.scalar.dma_start(out=sin_sb[:], in_=sin.rearrange("(p j) d -> p (j d)", j=2))
+        raw_x = load_slab("x", x_rows)
+        raw_w = [
+            [load_slab("wq_even", wq_rows[0]), load_slab("wq_odd", wq_rows[1])],
+            [load_slab("wk_even", wk_rows[0]), load_slab("wk_odd", wk_rows[1])],
+        ]
+
+        identity = keep.tile([P, P], F32)
+        make_identity(nc, identity[:])
+
+        sin_even = sin_sb[:].rearrange("p (n c) -> p n c", c=2)[:, :, 0:1]
+        nc.gpsimd.tensor_scalar_mul(out=sin_even, in0=sin_even, scalar1=-1.0)
+
+        def quantise_slab(raw, codes, scales):
+            words = raw[:].bitcast(F32)
+            flipped = flip_banks.tile([P, 2, SLAB], F32)
+            for j in range(2):
+                for u in range(2):
+                    nc.tensor.transpose(
+                        out=flipped[:, u, j * P : (j + 1) * P],
+                        in_=words[:, j * WORDS + u * P : j * WORDS + (u + 1) * P],
+                        identity=identity[:],
+                    )
+            grouped = stage.tile([P, 2 * SLAB], F32, align_bytes=64)
+            nc.scalar.copy(
+                out=grouped[:].rearrange("p (r u) -> p r u", u=2),
+                in_=flipped[:].rearrange("p u r -> p r u"),
+            )
+            nc.vector.quantize_mx(
+                out=codes.bitcast(FP8X4), scales=scales, in_=grouped[:].bitcast(BF16)
+            )
+
+        x_codes = keep.tile([P, SLAB], U32, align_bytes=64)
+        x_scales = keep.tile([P, SLAB], U8, align_bytes=64)
+        quantise_slab(raw_x, x_codes[:], x_scales[:])
+
+        w_codes = []
+        w_scales = []
+        for w in range(2):
+            codes = keep.tile([P, 2 * SLAB], U32, name="w_codes%d" % w, align_bytes=64)
+            scales = keep.tile([P, 2 * SLAB], U8, name="w_scales%d" % w, align_bytes=64)
+            for c in range(2):
+                half = slice(c * SLAB, (c + 1) * SLAB)
+                quantise_slab(raw_w[w][c], codes[:, half], scales[:, half])
+            w_codes.append(codes)
+            w_scales.append(scales)
+
+        for w, (out, scale) in enumerate(((out_0, 1.0), (out_1, SCALING))):
+            out_tiles = out.rearrange("b h (p j) d -> j p (b h) d", j=2)
+            for j in range(2):
+                straight = product_banks.tile([P, 2 * SLAB], F32)
+                crossed = product_banks.tile([P, 2 * SLAB], F32)
+                for c in range(2):
+                    for bank, place in ((straight, c), (crossed, 1 - c)):
+                        nc.tensor.matmul_mx(
+                            out=bank[:, place * SLAB : (place + 1) * SLAB],
+                            lhsT=x_codes[:, j * P : (j + 1) * P].bitcast(FP8X4),
+                            lhsT_scale=x_scales[:, j * P : (j + 1) * P],
+                            rhs=w_codes[w][:, c * SLAB : (c + 1) * SLAB].bitcast(FP8X4),
+                            rhs_scale=w_scales[w][:, c * SLAB : (c + 1) * SLAB],
+                            start=True,
+                            stop=True,
+                        )
+
+                parts = []
+                for label, bank, table in (("cos", straight, cos_sb), ("sin", crossed, sin_sb)):
+                    part = rotated.tile([P, HEADS * HEAD_DIM], F32, name=label + "_part")
+                    nc.vector.scalar_tensor_tensor(
+                        out=part[:].rearrange("p (h i c) -> p h i c", h=HEADS, c=2),
+                        in0=bank[:].rearrange("p (c h i) -> p h i c", c=2, h=HEADS),
+                        scalar=scale,
+                        in1=table[:, j * HEAD_DIM : (j + 1) * HEAD_DIM]
+                        .rearrange("p (i c) -> p i c", c=2)
+                        .unsqueeze(1)
+                        .to_broadcast([P, HEADS, PAIRS, 2]),
+                        op0=MULT,
+                        op1=MULT,
+                    )
+                    parts.append(part)
+
+                last = w == 1 and j == 1
+                adder = nc.vector if last else nc.gpsimd
+                adder.tensor_tensor(out=parts[0][:], in0=parts[0][:], in1=parts[1][:], op=ADD)
+                nc.sync.dma_start(
+                    out=out_tiles[j], in_=parts[0][:].rearrange("p (h d) -> p h d", h=HEADS)
+                )

@@ -16,10 +16,10 @@ T = 256
 E = 512
 HEADS = 4
 HEAD_DIM = 128
-PAIRS = HEAD_DIM // 2
 SCALING = HEAD_DIM**-0.5
 WORDS = E // 2
 SLAB = 2 * P
+SLAB_HEADS = SLAB // HEAD_DIM
 FLOPS = 2 * T * E * (2 * E)
 
 
@@ -32,26 +32,25 @@ def tile_nucleusxmultiscaleretention_pa_s_kernel(
         stage = ctx.enter_context(tc.tile_pool(name="stage", bufs=3))
         rotated = ctx.enter_context(tc.tile_pool(name="rotated", bufs=4))
         flip_banks = ctx.enter_context(tc.psum_pool(name="flip_banks", bufs=4))
-        product_banks = ctx.enter_context(tc.psum_pool(name="product_banks", bufs=2))
-
-        x_rows = hidden_states.flatten_outer_dims().rearrange("(p j) k -> p j k", j=2)
-        wq_rows = wq.rearrange("(j p c) k -> c p j k", j=2, c=2)
-        wk_rows = wk.rearrange("(j p c) k -> c p j k", j=2, c=2)
+        product_banks = ctx.enter_context(tc.psum_pool(name="product_banks", bufs=4))
 
         def load_slab(label, rows):
             raw = keep.tile([P, 2 * E], BF16, name="raw_" + label)
-            nc.sync.dma_start(out=raw[:].rearrange("p (j k) -> p j k", j=2), in_=rows)
+            nc.sync.dma_start(out=raw[:], in_=rows.rearrange("(p j) k -> p (j k)", j=2))
             return raw
 
-        cos_sb = keep.tile([P, 2 * HEAD_DIM], BF16)
-        sin_sb = keep.tile([P, 2 * HEAD_DIM], BF16)
-        nc.scalar.dma_start(out=cos_sb[:], in_=cos.rearrange("(p j) d -> p (j d)", j=2))
-        nc.scalar.dma_start(out=sin_sb[:], in_=sin.rearrange("(p j) d -> p (j d)", j=2))
-        raw_x = load_slab("x", x_rows)
-        raw_w = [
-            [load_slab("wq_even", wq_rows[0]), load_slab("wq_odd", wq_rows[1])],
-            [load_slab("wk_even", wk_rows[0]), load_slab("wk_odd", wk_rows[1])],
-        ]
+        def load_table(label, table):
+            loaded = keep.tile([P, 2 * HEAD_DIM], BF16, name=label)
+            nc.sync.dma_start(out=loaded[:], in_=table.rearrange("(p j) d -> p (j d)", j=2))
+            return loaded
+
+        raw_x = load_slab("x", hidden_states.flatten_outer_dims())
+        raw_w = [load_slab("wq0", wq[0:SLAB, :])]
+        cos_sb = load_table("cos_sb", cos)
+        sin_sb = load_table("sin_sb", sin)
+        raw_w.append(load_slab("wq1", wq[SLAB : 2 * SLAB, :]))
+        raw_w.append(load_slab("wk0", wk[0:SLAB, :]))
+        raw_w.append(load_slab("wk1", wk[SLAB : 2 * SLAB, :]))
 
         identity = keep.tile([P, P], F32)
         make_identity(nc, identity[:])
@@ -59,76 +58,103 @@ def tile_nucleusxmultiscaleretention_pa_s_kernel(
         sin_even = sin_sb[:].rearrange("p (n c) -> p n c", c=2)[:, :, 0:1]
         nc.gpsimd.tensor_scalar_mul(out=sin_even, in0=sin_even, scalar1=-1.0)
 
-        def quantise_slab(raw, codes, scales):
+        def transpose_half(raw, j, out):
             words = raw[:].bitcast(F32)
-            flipped = flip_banks.tile([P, 2, SLAB], F32)
-            for j in range(2):
-                for u in range(2):
-                    nc.tensor.transpose(
-                        out=flipped[:, u, j * P : (j + 1) * P],
-                        in_=words[:, j * WORDS + u * P : j * WORDS + (u + 1) * P],
-                        identity=identity[:],
-                    )
-            grouped = stage.tile([P, 2 * SLAB], F32, align_bytes=64)
-            nc.scalar.copy(
-                out=grouped[:].rearrange("p (r u) -> p r u", u=2),
-                in_=flipped[:].rearrange("p u r -> p r u"),
-            )
-            nc.vector.quantize_mx(
-                out=codes.bitcast(FP8X4), scales=scales, in_=grouped[:].bitcast(BF16)
-            )
+            for u in range(2):
+                nc.tensor.transpose(
+                    out=out[:, u, :],
+                    in_=words[:, j * WORDS + u * P : j * WORDS + (u + 1) * P],
+                    identity=identity[:],
+                )
 
         x_codes = keep.tile([P, SLAB], U32, align_bytes=64)
         x_scales = keep.tile([P, SLAB], U8, align_bytes=64)
-        quantise_slab(raw_x, x_codes[:], x_scales[:])
+        x_grouped = []
+        for j in range(2):
+            flipped = flip_banks.tile([P, 2, SLAB], F32)
+            transpose_half(raw_x, j, flipped[:, :, 0:P])
+            grouped = keep.tile([P, 2 * P], F32, name="x_grouped%d" % j, align_bytes=64)
+            copy = nc.scalar.copy if j == 0 else nc.vector.tensor_copy
+            copy(
+                out=grouped[:].rearrange("p (r u) -> p r u", u=2),
+                in_=flipped[:, :, 0:P].rearrange("p u r -> p r u"),
+            )
+            x_grouped.append(grouped)
+        for j in range(2):
+            half = slice(j * P, (j + 1) * P)
+            nc.vector.quantize_mx(
+                out=x_codes[:, half].bitcast(FP8X4),
+                scales=x_scales[:, half],
+                in_=x_grouped[j][:].bitcast(BF16),
+            )
 
-        w_codes = []
-        w_scales = []
-        for w in range(2):
-            codes = keep.tile([P, 2 * SLAB], U32, name="w_codes%d" % w, align_bytes=64)
-            scales = keep.tile([P, 2 * SLAB], U8, name="w_scales%d" % w, align_bytes=64)
-            for c in range(2):
-                half = slice(c * SLAB, (c + 1) * SLAB)
-                quantise_slab(raw_w[w][c], codes[:, half], scales[:, half])
-            w_codes.append(codes)
-            w_scales.append(scales)
-
-        for w, (out, scale) in enumerate(((out_0, 1.0), (out_1, SCALING))):
-            out_tiles = out.rearrange("b h (p j) d -> j p (b h) d", j=2)
+        def prepare_weights(s):
+            flipped = flip_banks.tile([P, 2, SLAB], F32)
             for j in range(2):
-                straight = product_banks.tile([P, 2 * SLAB], F32)
-                crossed = product_banks.tile([P, 2 * SLAB], F32)
-                for c in range(2):
-                    for bank, place in ((straight, c), (crossed, 1 - c)):
-                        nc.tensor.matmul_mx(
-                            out=bank[:, place * SLAB : (place + 1) * SLAB],
-                            lhsT=x_codes[:, j * P : (j + 1) * P].bitcast(FP8X4),
-                            lhsT_scale=x_scales[:, j * P : (j + 1) * P],
-                            rhs=w_codes[w][:, c * SLAB : (c + 1) * SLAB].bitcast(FP8X4),
-                            rhs_scale=w_scales[w][:, c * SLAB : (c + 1) * SLAB],
-                            start=True,
-                            stop=True,
-                        )
+                transpose_half(raw_w[s], j, flipped[:, :, j * P : (j + 1) * P])
+            grouped = stage.tile([P, 2 * SLAB], F32, align_bytes=64)
+            nc.scalar.copy(
+                out=grouped[:].rearrange("p (r j u) -> p r j u", j=2, u=2),
+                in_=flipped[:].rearrange("p u (j r) -> p r j u", j=2),
+            )
+            codes = keep.tile([P, SLAB], U32, name="w_codes%d" % s, align_bytes=64)
+            scales = keep.tile([P, SLAB], U8, name="w_scales%d" % s, align_bytes=64)
+            nc.vector.quantize_mx(
+                out=codes[:].bitcast(FP8X4), scales=scales[:], in_=grouped[:].bitcast(BF16)
+            )
+            return codes, scales
 
-                parts = []
-                for label, bank, table in (("cos", straight, cos_sb), ("sin", crossed, sin_sb)):
-                    part = rotated.tile([P, HEADS * HEAD_DIM], F32, name=label + "_part")
-                    nc.vector.scalar_tensor_tensor(
-                        out=part[:].rearrange("p (h i c) -> p h i c", h=HEADS, c=2),
-                        in0=bank[:].rearrange("p (c h i) -> p h i c", c=2, h=HEADS),
-                        scalar=scale,
-                        in1=table[:, j * HEAD_DIM : (j + 1) * HEAD_DIM]
-                        .rearrange("p (i c) -> p i c", c=2)
-                        .unsqueeze(1)
-                        .to_broadcast([P, HEADS, PAIRS, 2]),
-                        op0=MULT,
-                        op1=MULT,
+        def multiply(codes, scales):
+            bank = product_banks.tile([P, SLAB_HEADS, 2, HEAD_DIM], F32)
+            for h in range(SLAB_HEADS):
+                head = slice(h * HEAD_DIM, (h + 1) * HEAD_DIM)
+                for j in range(2):
+                    half = slice(j * P, (j + 1) * P)
+                    nc.tensor.matmul_mx(
+                        out=bank[:, h, j, :],
+                        lhsT=x_codes[:, half].bitcast(FP8X4),
+                        lhsT_scale=x_scales[:, half],
+                        rhs=codes[:, head].bitcast(FP8X4),
+                        rhs_scale=scales[:, head],
+                        start=True,
+                        stop=True,
                     )
-                    parts.append(part)
+            return bank
 
-                last = w == 1 and j == 1
-                adder = nc.vector if last else nc.gpsimd
-                adder.tensor_tensor(out=parts[0][:], in0=parts[0][:], in1=parts[1][:], op=ADD)
-                nc.sync.dma_start(
-                    out=out_tiles[j], in_=parts[0][:].rearrange("p (h d) -> p h d", h=HEADS)
+        def rotate(s, bank):
+            out, scale = ((out_0, 1.0), (out_1, SCALING))[s // 2]
+            straight = bank[:].rearrange("p h j (i c) -> p h (j i) c", c=2)
+            parts = []
+            for label, read, table in (
+                ("cos", straight, cos_sb),
+                ("sin", straight[:, :, :, ::-1], sin_sb),
+            ):
+                part = rotated.tile([P, SLAB_HEADS * 2 * HEAD_DIM], F32, name=label + "_part")
+                nc.vector.scalar_tensor_tensor(
+                    out=part[:].rearrange("p (h n c) -> p h n c", h=SLAB_HEADS, c=2),
+                    in0=read,
+                    scalar=scale,
+                    in1=table[:]
+                    .rearrange("p (n c) -> p n c", c=2)
+                    .unsqueeze(1)
+                    .to_broadcast([P, SLAB_HEADS, 2 * HEAD_DIM // 2, 2]),
+                    op0=MULT,
+                    op1=MULT,
                 )
+                parts.append(part)
+            adder = nc.vector if s == 3 else nc.gpsimd
+            adder.tensor_tensor(out=parts[0][:], in0=parts[0][:], in1=parts[1][:], op=ADD)
+            first = (s % 2) * SLAB_HEADS
+            nc.sync.dma_start(
+                out=out.rearrange("b h (p j) d -> p (b h) (j d)", j=2)[
+                    :, first : first + SLAB_HEADS, :
+                ],
+                in_=parts[0][:].rearrange("p (h n) -> p h n", h=SLAB_HEADS),
+            )
+
+        bank = multiply(*prepare_weights(0))
+        for s in range(1, 4):
+            ready = prepare_weights(s)
+            rotate(s - 1, bank)
+            bank = multiply(*ready)
+        rotate(3, bank)

@@ -17,9 +17,7 @@ E = 512
 HEADS = 4
 HEAD_DIM = 128
 SCALING = HEAD_DIM**-0.5
-WORDS = E // 2
-SLAB = 2 * P
-SLAB_HEADS = SLAB // HEAD_DIM
+UNITS = ((0, 0, 1), (0, 1, 1), (0, 2, 2), (1, 0, 2), (1, 2, 1), (1, 3, 1))
 FLOPS = 2 * T * E * (2 * E)
 
 
@@ -34,9 +32,17 @@ def tile_nucleusxmultiscaleretention_pa_s_kernel(
         flip_banks = ctx.enter_context(tc.psum_pool(name="flip_banks", bufs=4))
         product_banks = ctx.enter_context(tc.psum_pool(name="product_banks", bufs=4))
 
-        def load_slab(label, rows):
-            raw = keep.tile([P, 2 * E], BF16, name="raw_" + label)
-            nc.sync.dma_start(out=raw[:], in_=rows.rearrange("(p j) k -> p (j k)", j=2))
+        def load_unit(i):
+            w, first, n = UNITS[i]
+            rows = (wq, wk)[w][first * HEAD_DIM : (first + n) * HEAD_DIM, :]
+            raw = keep.tile([P, n * E], BF16, name="raw_w%d" % i)
+            nc.sync.dma_start(out=raw[:], in_=rows.rearrange("(p j) k -> p (j k)", j=n))
+            return raw
+
+        def load_positions(j):
+            rows = hidden_states.flatten_outer_dims().rearrange("(p j) k -> j p k", j=2)[j]
+            raw = keep.tile([P, E], BF16, name="raw_x%d" % j)
+            nc.sync.dma_start(out=raw[:], in_=rows)
             return raw
 
         def load_table(label, table):
@@ -44,69 +50,88 @@ def tile_nucleusxmultiscaleretention_pa_s_kernel(
             nc.sync.dma_start(out=loaded[:], in_=table.rearrange("(p j) d -> p (j d)", j=2))
             return loaded
 
-        raw_x = load_slab("x", hidden_states.flatten_outer_dims())
-        raw_w = [load_slab("wq0", wq[0:SLAB, :])]
+        raw_w = [load_unit(0)]
+        raw_x = [load_positions(0), load_positions(1)]
+        raw_w.extend([load_unit(1), load_unit(2)])
         cos_sb = load_table("cos_sb", cos)
         sin_sb = load_table("sin_sb", sin)
-        raw_w.append(load_slab("wq1", wq[SLAB : 2 * SLAB, :]))
-        raw_w.append(load_slab("wk0", wk[0:SLAB, :]))
-        raw_w.append(load_slab("wk1", wk[SLAB : 2 * SLAB, :]))
+        raw_w.extend([load_unit(i) for i in range(3, len(UNITS))])
 
         identity = keep.tile([P, P], F32)
         make_identity(nc, identity[:])
 
         sin_even = sin_sb[:].rearrange("p (n c) -> p n c", c=2)[:, :, 0:1]
-        nc.gpsimd.tensor_scalar_mul(out=sin_even, in0=sin_even, scalar1=-1.0)
+        nc.gpsimd.tensor_scalar(
+            out=sin_even, in0=sin_even, scalar1=-1.0, scalar2=0.0, op0=MULT, op1=ADD
+        )
 
-        def transpose_half(raw, j, out):
-            words = raw[:].bitcast(F32)
+        def transpose_rows(raw, out):
+            words = raw.bitcast(F32)
             for u in range(2):
                 nc.tensor.transpose(
                     out=out[:, u, :],
-                    in_=words[:, j * WORDS + u * P : j * WORDS + (u + 1) * P],
+                    in_=words[:, u * P : (u + 1) * P],
                     identity=identity[:],
                 )
 
-        x_codes = keep.tile([P, SLAB], U32, align_bytes=64)
-        x_scales = keep.tile([P, SLAB], U8, align_bytes=64)
+        x_codes = keep.tile([P, T], U32, align_bytes=64)
+        x_scales = keep.tile([P, T], U8, align_bytes=64)
         x_grouped = []
-        for j in range(2):
-            flipped = flip_banks.tile([P, 2, SLAB], F32)
-            transpose_half(raw_x, j, flipped[:, :, 0:P])
-            grouped = keep.tile([P, 2 * P], F32, name="x_grouped%d" % j, align_bytes=64)
-            copy = nc.scalar.copy if j == 0 else nc.vector.tensor_copy
-            copy(
-                out=grouped[:].rearrange("p (r u) -> p r u", u=2),
-                in_=flipped[:, :, 0:P].rearrange("p u r -> p r u"),
-            )
-            x_grouped.append(grouped)
-        for j in range(2):
-            half = slice(j * P, (j + 1) * P)
-            nc.vector.quantize_mx(
-                out=x_codes[:, half].bitcast(FP8X4),
-                scales=x_scales[:, half],
-                in_=x_grouped[j][:].bitcast(BF16),
-            )
 
-        def prepare_weights(s):
-            flipped = flip_banks.tile([P, 2, SLAB], F32)
+        def transpose_positions():
             for j in range(2):
-                transpose_half(raw_w[s], j, flipped[:, :, j * P : (j + 1) * P])
-            grouped = stage.tile([P, 2 * SLAB], F32, align_bytes=64)
-            nc.scalar.copy(
-                out=grouped[:].rearrange("p (r j u) -> p r j u", j=2, u=2),
-                in_=flipped[:].rearrange("p u (j r) -> p r j u", j=2),
-            )
-            codes = keep.tile([P, SLAB], U32, name="w_codes%d" % s, align_bytes=64)
-            scales = keep.tile([P, SLAB], U8, name="w_scales%d" % s, align_bytes=64)
-            nc.vector.quantize_mx(
-                out=codes[:].bitcast(FP8X4), scales=scales[:], in_=grouped[:].bitcast(BF16)
-            )
-            return codes, scales
+                flipped = flip_banks.tile([P, 2, P], F32)
+                transpose_rows(raw_x[j][:], flipped[:])
+                grouped = keep.tile([P, 2 * P], F32, name="x_grouped%d" % j, align_bytes=64)
+                copy = nc.scalar.copy if j == 0 else nc.vector.tensor_copy
+                copy(
+                    out=grouped[:].rearrange("p (r u) -> p r u", u=2),
+                    in_=flipped[:].rearrange("p u r -> p r u"),
+                )
+                x_grouped.append(grouped)
 
-        def multiply(codes, scales):
-            bank = product_banks.tile([P, SLAB_HEADS, 2, HEAD_DIM], F32)
-            for h in range(SLAB_HEADS):
+        def quantise_positions():
+            for j in range(2):
+                half = slice(j * P, (j + 1) * P)
+                nc.vector.quantize_mx(
+                    out=x_codes[:, half].bitcast(FP8X4),
+                    scales=x_scales[:, half],
+                    in_=x_grouped[j][:].bitcast(BF16),
+                )
+
+        flipped_w, grouped_w, codes_w, scales_w, banks = {}, {}, {}, {}, {}
+
+        def transpose_weights(i):
+            n = UNITS[i][2]
+            flipped = flip_banks.tile([P, 2, n * P], F32)
+            for j in range(n):
+                transpose_rows(
+                    raw_w[i][:, j * E : (j + 1) * E], flipped[:, :, j * P : (j + 1) * P]
+                )
+            flipped_w[i] = flipped
+
+        def group_weights(i):
+            n = UNITS[i][2]
+            grouped = stage.tile([P, 2 * n * P], F32, align_bytes=64)
+            nc.scalar.copy(
+                out=grouped[:].rearrange("p (r j u) -> p r j u", j=n, u=2),
+                in_=flipped_w[i][:].rearrange("p u (j r) -> p r j u", j=n),
+            )
+            grouped_w[i] = grouped
+
+        def quantise_weights(i):
+            n = UNITS[i][2]
+            codes = keep.tile([P, n * P], U32, name="w_codes%d" % i, align_bytes=64)
+            scales = keep.tile([P, n * P], U8, name="w_scales%d" % i, align_bytes=64)
+            nc.vector.quantize_mx(
+                out=codes[:].bitcast(FP8X4), scales=scales[:], in_=grouped_w[i][:].bitcast(BF16)
+            )
+            codes_w[i], scales_w[i] = codes, scales
+
+        def multiply(i):
+            n = UNITS[i][2]
+            bank = product_banks.tile([P, n, 2, HEAD_DIM], F32)
+            for h in range(n):
                 head = slice(h * HEAD_DIM, (h + 1) * HEAD_DIM)
                 for j in range(2):
                     half = slice(j * P, (j + 1) * P)
@@ -114,47 +139,60 @@ def tile_nucleusxmultiscaleretention_pa_s_kernel(
                         out=bank[:, h, j, :],
                         lhsT=x_codes[:, half].bitcast(FP8X4),
                         lhsT_scale=x_scales[:, half],
-                        rhs=codes[:, head].bitcast(FP8X4),
-                        rhs_scale=scales[:, head],
+                        rhs=codes_w[i][:, head].bitcast(FP8X4),
+                        rhs_scale=scales_w[i][:, head],
                         start=True,
                         stop=True,
                     )
-            return bank
+            banks[i] = bank
 
-        def rotate(s, bank):
-            out, scale = ((out_0, 1.0), (out_1, SCALING))[s // 2]
-            straight = bank[:].rearrange("p h j (i c) -> p h (j i) c", c=2)
+        def rotate(i):
+            w, first, n = UNITS[i]
+            out, scale = ((out_0, 1.0), (out_1, SCALING))[w]
+            straight = banks[i][:].rearrange("p h j (i c) -> p h (j i) c", c=2)
             parts = []
             for label, read, table in (
                 ("cos", straight, cos_sb),
                 ("sin", straight[:, :, :, ::-1], sin_sb),
             ):
-                part = rotated.tile([P, SLAB_HEADS * 2 * HEAD_DIM], F32, name=label + "_part")
+                part = rotated.tile([P, n * 2 * HEAD_DIM], F32, name=label + "_part")
                 nc.vector.scalar_tensor_tensor(
-                    out=part[:].rearrange("p (h n c) -> p h n c", h=SLAB_HEADS, c=2),
+                    out=part[:].rearrange("p (h n c) -> p h n c", h=n, c=2),
                     in0=read,
                     scalar=scale,
                     in1=table[:]
                     .rearrange("p (n c) -> p n c", c=2)
                     .unsqueeze(1)
-                    .to_broadcast([P, SLAB_HEADS, 2 * HEAD_DIM // 2, 2]),
+                    .to_broadcast([P, n, HEAD_DIM, 2]),
                     op0=MULT,
                     op1=MULT,
                 )
                 parts.append(part)
-            adder = nc.vector if s == 3 else nc.gpsimd
+            adder = nc.vector if i == len(UNITS) - 1 else nc.gpsimd
             adder.tensor_tensor(out=parts[0][:], in0=parts[0][:], in1=parts[1][:], op=ADD)
-            first = (s % 2) * SLAB_HEADS
             nc.sync.dma_start(
-                out=out.rearrange("b h (p j) d -> p (b h) (j d)", j=2)[
-                    :, first : first + SLAB_HEADS, :
-                ],
-                in_=parts[0][:].rearrange("p (h n) -> p h n", h=SLAB_HEADS),
+                out=out.rearrange("b h (p j) d -> p (b h) (j d)", j=2)[:, first : first + n, :],
+                in_=parts[0][:].rearrange("p (h n) -> p h n", h=n),
             )
 
-        bank = multiply(*prepare_weights(0))
-        for s in range(1, 4):
-            ready = prepare_weights(s)
-            rotate(s - 1, bank)
-            bank = multiply(*ready)
-        rotate(3, bank)
+        last = len(UNITS) - 1
+        with tc.manual_schedule():
+            transpose_weights(0)
+            group_weights(0)
+            quantise_weights(0)
+            transpose_positions()
+            for i in (1, 2):
+                transpose_weights(i)
+                group_weights(i)
+            quantise_positions()
+            quantise_weights(1)
+            multiply(0)
+            for i in range(last + 1):
+                if i + 3 <= last:
+                    transpose_weights(i + 3)
+                    group_weights(i + 3)
+                if i + 1 <= last:
+                    multiply(i + 1)
+                rotate(i)
+                if i + 2 <= last:
+                    quantise_weights(i + 2)

@@ -147,8 +147,8 @@ def tile_nucleusxmultiscaleretention_pa_s_kernel(
             banks[i] = bank
 
         def rotate(i):
-            w, first, n = UNITS[i]
-            out, scale = ((out_0, 1.0), (out_1, SCALING))[w]
+            w, n = UNITS[i][0], UNITS[i][2]
+            scale = (1.0, SCALING)[w]
             straight = banks[i][:].rearrange("p h j (i c) -> p h (j i) c", c=2)
             parts = []
             for label, read, table in (
@@ -168,7 +168,11 @@ def tile_nucleusxmultiscaleretention_pa_s_kernel(
                     op1=MULT,
                 )
                 parts.append(part)
-            adder = nc.vector if i == len(UNITS) - 1 else nc.gpsimd
+            return parts
+
+        def add_and_store(i, adder, parts):
+            w, first, n = UNITS[i]
+            out = (out_0, out_1)[w]
             adder.tensor_tensor(out=parts[0][:], in0=parts[0][:], in1=parts[1][:], op=ADD)
             nc.sync.dma_start(
                 out=out.rearrange("b h (p j) d -> p (b h) (j d)", j=2)[:, first : first + n, :],
@@ -187,12 +191,19 @@ def tile_nucleusxmultiscaleretention_pa_s_kernel(
             quantise_positions()
             quantise_weights(1)
             multiply(0)
+            parts = {}
             for i in range(last + 1):
                 if i + 3 <= last:
                     transpose_weights(i + 3)
                     group_weights(i + 3)
                 if i + 1 <= last:
                     multiply(i + 1)
-                rotate(i)
-                if i + 2 <= last:
+                parts[i] = rotate(i)
+                if i < last - 1:
+                    add_and_store(i, nc.gpsimd, parts[i])
+                if i + 2 < last:
                     quantise_weights(i + 2)
+                if i + 3 == last:
+                    quantise_weights(last)
+            for i in (last - 1, last):
+                add_and_store(i, nc.vector, parts[i])

@@ -17,7 +17,8 @@ E = 512
 HEADS = 4
 HEAD_DIM = 128
 SCALING = HEAD_DIM**-0.5
-UNITS = ((0, 0, 1), (0, 1, 1), (0, 2, 2), (1, 0, 2), (1, 2, 1), (1, 3, 1))
+SLABS = ((0, 1), (1, 1), (2, 2), (4, 2), (6, 2))
+SLAB_OF_HEAD = [i for i, (first, n) in enumerate(SLABS) for h in range(n)]
 FLOPS = 2 * T * E * (2 * E)
 
 
@@ -28,13 +29,14 @@ def tile_nucleusxmultiscaleretention_pa_s_kernel(
     with ExitStack() as ctx:
         keep = ctx.enter_context(tc.tile_pool(name="keep", bufs=1))
         stage = ctx.enter_context(tc.tile_pool(name="stage", bufs=3))
-        rotated = ctx.enter_context(tc.tile_pool(name="rotated", bufs=4))
+        rotated = ctx.enter_context(tc.tile_pool(name="rotated", bufs=2 * HEADS))
         flip_banks = ctx.enter_context(tc.psum_pool(name="flip_banks", bufs=4))
         product_banks = ctx.enter_context(tc.psum_pool(name="product_banks", bufs=4))
 
-        def load_unit(i):
-            w, first, n = UNITS[i]
-            rows = (wq, wk)[w][first * HEAD_DIM : (first + n) * HEAD_DIM, :]
+        def load_weights(i):
+            first, n = SLABS[i]
+            row = first % HEADS * HEAD_DIM
+            rows = (wq, wk)[first // HEADS][row : row + n * HEAD_DIM, :]
             raw = keep.tile([P, n * E], BF16, name="raw_w%d" % i)
             nc.sync.dma_start(out=raw[:], in_=rows.rearrange("(p j) k -> p (j k)", j=n))
             return raw
@@ -50,20 +52,19 @@ def tile_nucleusxmultiscaleretention_pa_s_kernel(
             nc.sync.dma_start(out=loaded[:], in_=table.rearrange("(p j) d -> p (j d)", j=2))
             return loaded
 
-        raw_w = [load_unit(0)]
+        raw_w = [load_weights(0)]
         raw_x = [load_positions(0), load_positions(1)]
-        raw_w.extend([load_unit(1), load_unit(2)])
+        raw_w.extend([load_weights(1), load_weights(2)])
         cos_sb = load_table("cos_sb", cos)
         sin_sb = load_table("sin_sb", sin)
-        raw_w.extend([load_unit(i) for i in range(3, len(UNITS))])
+        raw_w.extend([load_weights(i) for i in range(3, len(SLABS))])
 
         identity = keep.tile([P, P], F32)
         make_identity(nc, identity[:])
 
-        sin_even = sin_sb[:].rearrange("p (n c) -> p n c", c=2)[:, :, 0:1]
-        nc.gpsimd.tensor_scalar(
-            out=sin_even, in0=sin_even, scalar1=-1.0, scalar2=0.0, op0=MULT, op1=ADD
-        )
+        def negate_even_sines():
+            sin_even = sin_sb[:].rearrange("p (n c) -> p n c", c=2)[:, :, 0:1]
+            nc.scalar.mul(out=sin_even, in_=sin_even, mul=-1.0)
 
         def transpose_rows(raw, out):
             words = raw.bitcast(F32)
@@ -102,7 +103,7 @@ def tile_nucleusxmultiscaleretention_pa_s_kernel(
         flipped_w, grouped_w, codes_w, scales_w, banks = {}, {}, {}, {}, {}
 
         def transpose_weights(i):
-            n = UNITS[i][2]
+            n = SLABS[i][1]
             flipped = flip_banks.tile([P, 2, n * P], F32)
             for j in range(n):
                 transpose_rows(
@@ -111,7 +112,7 @@ def tile_nucleusxmultiscaleretention_pa_s_kernel(
             flipped_w[i] = flipped
 
         def group_weights(i):
-            n = UNITS[i][2]
+            n = SLABS[i][1]
             grouped = stage.tile([P, 2 * n * P], F32, align_bytes=64)
             nc.scalar.copy(
                 out=grouped[:].rearrange("p (r j u) -> p r j u", j=n, u=2),
@@ -120,7 +121,7 @@ def tile_nucleusxmultiscaleretention_pa_s_kernel(
             grouped_w[i] = grouped
 
         def quantise_weights(i):
-            n = UNITS[i][2]
+            n = SLABS[i][1]
             codes = keep.tile([P, n * P], U32, name="w_codes%d" % i, align_bytes=64)
             scales = keep.tile([P, n * P], U8, name="w_scales%d" % i, align_bytes=64)
             nc.vector.quantize_mx(
@@ -128,82 +129,74 @@ def tile_nucleusxmultiscaleretention_pa_s_kernel(
             )
             codes_w[i], scales_w[i] = codes, scales
 
-        def multiply(i):
-            n = UNITS[i][2]
-            bank = product_banks.tile([P, n, 2, HEAD_DIM], F32)
-            for h in range(n):
-                head = slice(h * HEAD_DIM, (h + 1) * HEAD_DIM)
-                for j in range(2):
-                    half = slice(j * P, (j + 1) * P)
-                    nc.tensor.matmul_mx(
-                        out=bank[:, h, j, :],
-                        lhsT=x_codes[:, half].bitcast(FP8X4),
-                        lhsT_scale=x_scales[:, half],
-                        rhs=codes_w[i][:, head].bitcast(FP8X4),
-                        rhs_scale=scales_w[i][:, head],
-                        start=True,
-                        stop=True,
-                    )
-            banks[i] = bank
+        def multiply(h):
+            i = SLAB_OF_HEAD[h]
+            column = (h - SLABS[i][0]) * HEAD_DIM
+            head = slice(column, column + HEAD_DIM)
+            bank = product_banks.tile([P, 2, HEAD_DIM], F32)
+            for j in range(2):
+                half = slice(j * P, (j + 1) * P)
+                nc.tensor.matmul_mx(
+                    out=bank[:, j, :],
+                    lhsT=x_codes[:, half].bitcast(FP8X4),
+                    lhsT_scale=x_scales[:, half],
+                    rhs=codes_w[i][:, head].bitcast(FP8X4),
+                    rhs_scale=scales_w[i][:, head],
+                    start=True,
+                    stop=True,
+                )
+            banks[h] = bank
 
-        def rotate(i):
-            w, n = UNITS[i][0], UNITS[i][2]
-            scale = (1.0, SCALING)[w]
-            straight = banks[i][:].rearrange("p h j (i c) -> p h (j i) c", c=2)
+        def rotate(h):
+            straight = banks[h][:].rearrange("p j (i c) -> p (j i) c", c=2)
             parts = []
             for label, read, table in (
                 ("cos", straight, cos_sb),
-                ("sin", straight[:, :, :, ::-1], sin_sb),
+                ("sin", straight[:, :, ::-1], sin_sb),
             ):
-                part = rotated.tile([P, n * 2 * HEAD_DIM], F32, name=label + "_part")
+                part = rotated.tile([P, 2 * HEAD_DIM], F32, name=label + "_part")
                 nc.vector.scalar_tensor_tensor(
-                    out=part[:].rearrange("p (h n c) -> p h n c", h=n, c=2),
+                    out=part[:].rearrange("p (n c) -> p n c", c=2),
                     in0=read,
-                    scalar=scale,
-                    in1=table[:]
-                    .rearrange("p (n c) -> p n c", c=2)
-                    .unsqueeze(1)
-                    .to_broadcast([P, n, HEAD_DIM, 2]),
+                    scalar=(1.0, SCALING)[h // HEADS],
+                    in1=table[:].rearrange("p (n c) -> p n c", c=2),
                     op0=MULT,
                     op1=MULT,
                 )
                 parts.append(part)
-            return parts
+            parts_of[h] = parts
 
-        def add_and_store(i, adder, parts):
-            w, first, n = UNITS[i]
-            out = (out_0, out_1)[w]
-            adder.tensor_tensor(out=parts[0][:], in0=parts[0][:], in1=parts[1][:], op=ADD)
-            nc.sync.dma_start(
-                out=out.rearrange("b h (p j) d -> p (b h) (j d)", j=2)[:, first : first + n, :],
-                in_=parts[0][:].rearrange("p (h n) -> p h n", h=n),
-            )
+        def add_and_store(h, adder):
+            cos_part, sin_part = parts_of[h]
+            adder.tensor_tensor(out=cos_part[:], in0=cos_part[:], in1=sin_part[:], op=ADD)
+            out = (out_0, out_1)[h // HEADS].rearrange("b h (p j) d -> p (b h) (j d)", j=2)
+            nc.sync.dma_start(out=out[:, h % HEADS, :], in_=cos_part[:])
 
-        last = len(UNITS) - 1
+        last = 2 * HEADS - 1
+        parts_of = {}
         with tc.manual_schedule():
             transpose_weights(0)
             group_weights(0)
             quantise_weights(0)
             transpose_positions()
-            for i in (1, 2):
-                transpose_weights(i)
-                group_weights(i)
+            transpose_weights(1)
+            group_weights(1)
+            negate_even_sines()
+            transpose_weights(2)
+            group_weights(2)
             quantise_positions()
             quantise_weights(1)
             multiply(0)
-            parts = {}
-            for i in range(last + 1):
-                if i + 3 <= last:
-                    transpose_weights(i + 3)
-                    group_weights(i + 3)
-                if i + 1 <= last:
-                    multiply(i + 1)
-                parts[i] = rotate(i)
-                if i < last - 1:
-                    add_and_store(i, nc.gpsimd, parts[i])
-                if i + 2 < last:
-                    quantise_weights(i + 2)
-                if i + 3 == last:
-                    quantise_weights(last)
-            for i in (last - 1, last):
-                add_and_store(i, nc.vector, parts[i])
+            for h in range(last + 1):
+                if h + 3 < len(SLABS):
+                    transpose_weights(h + 3)
+                    group_weights(h + 3)
+                if h < last:
+                    multiply(h + 1)
+                rotate(h)
+                if h < last - 1:
+                    add_and_store(h, nc.gpsimd)
+                if h + 2 < len(SLABS):
+                    quantise_weights(h + 2)
+            for h in (last - 1, last):
+                add_and_store(h, nc.vector)

@@ -19,6 +19,7 @@ HEAD_DIM = 128
 SCALING = HEAD_DIM**-0.5
 SLABS = ((0, 1), (1, 1), (2, 2), (4, 2), (6, 2))
 SLAB_OF_HEAD = [i for i, (first, n) in enumerate(SLABS) for h in range(n)]
+WARM_UP = 384
 FLOPS = 2 * T * E * (2 * E)
 
 
@@ -31,7 +32,8 @@ def tile_nucleusxmultiscaleretention_pa_s_kernel(
         stage = ctx.enter_context(tc.tile_pool(name="stage", bufs=3))
         rotated = ctx.enter_context(tc.tile_pool(name="rotated", bufs=2 * HEADS))
         flip_banks = ctx.enter_context(tc.psum_pool(name="flip_banks", bufs=4))
-        product_banks = ctx.enter_context(tc.psum_pool(name="product_banks", bufs=4))
+        product_banks = ctx.enter_context(tc.psum_pool(name="product_banks", bufs=3))
+        unread_banks = ctx.enter_context(tc.psum_pool(name="unread_banks", bufs=1))
 
         def load_weights(i):
             first, n = SLABS[i]
@@ -175,6 +177,16 @@ def tile_nucleusxmultiscaleretention_pa_s_kernel(
         last = 2 * HEADS - 1
         parts_of = {}
         with tc.manual_schedule():
+            zeros = keep.tile([P, P], F32)
+            nc.vector.memset(zeros[:], 0.0)
+            unread = unread_banks.tile([P, WARM_UP], F32)
+            nc.tensor.matmul(
+                out=unread[:],
+                lhsT=zeros[:],
+                rhs=zeros[:, 0:1].to_broadcast([P, WARM_UP]),
+                start=True,
+                stop=True,
+            )
             transpose_weights(0)
             group_weights(0)
             quantise_weights(0)

@@ -32,8 +32,7 @@ def tile_nucleusxmultiscaleretention_pa_s_kernel(
         stage = ctx.enter_context(tc.tile_pool(name="stage", bufs=3))
         rotated = ctx.enter_context(tc.tile_pool(name="rotated", bufs=2 * HEADS))
         flip_banks = ctx.enter_context(tc.psum_pool(name="flip_banks", bufs=4))
-        product_banks = ctx.enter_context(tc.psum_pool(name="product_banks", bufs=3))
-        unread_banks = ctx.enter_context(tc.psum_pool(name="unread_banks", bufs=1))
+        product_banks = ctx.enter_context(tc.psum_pool(name="product_banks", bufs=4))
 
         def load_weights(i):
             first, n = SLABS[i]
@@ -174,19 +173,23 @@ def tile_nucleusxmultiscaleretention_pa_s_kernel(
             out = (out_0, out_1)[h // HEADS].rearrange("b h (p j) d -> p (b h) (j d)", j=2)
             nc.sync.dma_start(out=out[:, h % HEADS, :], in_=cos_part[:])
 
+        def keep_tensor_busy(operand):
+            bank = product_banks.tile([P, WARM_UP], F32)
+            nc.tensor.matmul(
+                out=bank[:],
+                lhsT=operand[:, 0:P],
+                rhs=operand[:, 0:1].to_broadcast([P, WARM_UP]),
+                start=True,
+                stop=True,
+            )
+
         last = 2 * HEADS - 1
         parts_of = {}
         with tc.manual_schedule():
             zeros = keep.tile([P, P], F32)
             nc.vector.memset(zeros[:], 0.0)
-            unread = unread_banks.tile([P, WARM_UP], F32)
-            nc.tensor.matmul(
-                out=unread[:],
-                lhsT=zeros[:],
-                rhs=zeros[:, 0:1].to_broadcast([P, WARM_UP]),
-                start=True,
-                stop=True,
-            )
+            keep_tensor_busy(zeros[:].bitcast(BF16))
+            keep_tensor_busy(zeros[:])
             transpose_weights(0)
             group_weights(0)
             quantise_weights(0)

@@ -19,7 +19,6 @@ HEAD_DIM = 128
 SCALING = HEAD_DIM**-0.5
 SLABS = ((0, 1), (1, 1), (2, 2), (4, 2), (6, 2))
 SLAB_OF_HEAD = [i for i, (first, n) in enumerate(SLABS) for h in range(n)]
-WARM_UP = 384
 FLOPS = 2 * T * E * (2 * E)
 
 
@@ -173,12 +172,12 @@ def tile_nucleusxmultiscaleretention_pa_s_kernel(
             out = (out_0, out_1)[h // HEADS].rearrange("b h (p j) d -> p (b h) (j d)", j=2)
             nc.sync.dma_start(out=out[:, h % HEADS, :], in_=cos_part[:])
 
-        def keep_tensor_busy(operand):
-            bank = product_banks.tile([P, WARM_UP], F32)
+        def keep_tensor_busy(operand, columns):
+            bank = product_banks.tile([P, columns], F32)
             nc.tensor.matmul(
                 out=bank[:],
                 lhsT=operand[:, 0:P],
-                rhs=operand[:, 0:1].to_broadcast([P, WARM_UP]),
+                rhs=operand[:, 0:1].to_broadcast([P, columns]),
                 start=True,
                 stop=True,
             )
@@ -188,12 +187,13 @@ def tile_nucleusxmultiscaleretention_pa_s_kernel(
         with tc.manual_schedule():
             zeros = keep.tile([P, P], F32)
             nc.vector.memset(zeros[:], 0.0)
-            keep_tensor_busy(zeros[:].bitcast(BF16))
-            keep_tensor_busy(zeros[:])
+            keep_tensor_busy(zeros[:].bitcast(BF16), 128)
+            keep_tensor_busy(zeros[:], 416)
             transpose_weights(0)
             group_weights(0)
             quantise_weights(0)
             transpose_positions()
+            keep_tensor_busy(zeros[:], 256)
             transpose_weights(1)
             group_weights(1)
             negate_even_sines()

@@ -19,6 +19,8 @@ HEAD_DIM = 128
 SCALING = HEAD_DIM**-0.5
 SLABS = ((0, 1), (1, 1), (2, 2), (4, 2), (6, 2))
 SLAB_OF_HEAD = [i for i, (first, n) in enumerate(SLABS) for h in range(n)]
+TENSOR_ADDS = (4, 5, 6)
+GPSIMD_COSINES = (5,)
 FLOPS = 2 * T * E * (2 * E)
 
 
@@ -100,7 +102,7 @@ def tile_nucleusxmultiscaleretention_pa_s_kernel(
                     in_=x_grouped[j][:].bitcast(BF16),
                 )
 
-        flipped_w, grouped_w, codes_w, scales_w, banks = {}, {}, {}, {}, {}
+        flipped_w, grouped_w, codes_w, scales_w, banks, parts_of = {}, {}, {}, {}, {}, {}
 
         def transpose_weights(i):
             n = SLABS[i][1]
@@ -133,11 +135,11 @@ def tile_nucleusxmultiscaleretention_pa_s_kernel(
             i = SLAB_OF_HEAD[h]
             column = (h - SLABS[i][0]) * HEAD_DIM
             head = slice(column, column + HEAD_DIM)
-            bank = product_banks.tile([P, 2, HEAD_DIM], F32)
+            bank = product_banks.tile([P, 2 * HEAD_DIM], F32)
             for j in range(2):
                 half = slice(j * P, (j + 1) * P)
                 nc.tensor.matmul_mx(
-                    out=bank[:, j, :],
+                    out=bank[:, half],
                     lhsT=x_codes[:, half].bitcast(FP8X4),
                     lhsT_scale=x_scales[:, half],
                     rhs=codes_w[i][:, head].bitcast(FP8X4),
@@ -147,24 +149,36 @@ def tile_nucleusxmultiscaleretention_pa_s_kernel(
                 )
             banks[h] = bank
 
-        def rotate(h):
-            straight = banks[h][:].rearrange("p j (i c) -> p (j i) c", c=2)
-            parts = []
-            for label, read, table in (
-                ("cos", straight, cos_sb),
-                ("sin", straight[:, :, ::-1], sin_sb),
-            ):
-                part = rotated.tile([P, 2 * HEAD_DIM], F32, name=label + "_part")
-                nc.vector.scalar_tensor_tensor(
-                    out=part[:].rearrange("p (n c) -> p n c", c=2),
-                    in0=read,
-                    scalar=(1.0, SCALING)[h // HEADS],
-                    in1=table[:].rearrange("p (n c) -> p n c", c=2),
-                    op0=MULT,
-                    op1=MULT,
-                )
-                parts.append(part)
-            parts_of[h] = parts
+        def new_part(h, label):
+            part = rotated.tile([P, 2 * HEAD_DIM], F32, name=label + "_part")
+            parts_of.setdefault(h, []).append(part)
+            return part
+
+        def rotate(h, part_read_table):
+            part, read, table = part_read_table
+            nc.vector.scalar_tensor_tensor(
+                out=part[:].rearrange("p (n c) -> p n c", c=2),
+                in0=read,
+                scalar=(1.0, SCALING)[h // HEADS],
+                in1=table[:].rearrange("p (n c) -> p n c", c=2),
+                op0=MULT,
+                op1=MULT,
+            )
+
+        def cosine_on_gpsimd(h):
+            copied = rotated.tile([P, T], F32)
+            nc.scalar.copy(out=copied[:], in_=banks[h][:])
+            nc.gpsimd.tensor_tensor(
+                out=new_part(h, "cos")[:], in0=copied[:], in1=tables_t[:, 0, :], op=MULT
+            )
+
+        def cosine(h):
+            straight = banks[h][:].rearrange("p (n c) -> p n c", c=2)
+            rotate(h, (new_part(h, "cos"), straight, cos_sb))
+
+        def sine(h):
+            crossed = banks[h][:].rearrange("p (n c) -> p n c", c=2)[:, :, ::-1]
+            rotate(h, (new_part(h, "sin"), crossed, sin_sb))
 
         def add_and_store(h, adder):
             cos_part, sin_part = parts_of[h]
@@ -182,11 +196,81 @@ def tile_nucleusxmultiscaleretention_pa_s_kernel(
                 stop=True,
             )
 
-        last = 2 * HEADS - 1
-        parts_of = {}
+        exchange = keep.tile([P, P], F32)
+        identity_bf16 = keep.tile([P, P], BF16)
+        sin_exchanged = keep.tile([P, 2 * HEAD_DIM], BF16)
+        tables_t = keep.tile([P, 2, T], BF16)
+
+        def pairs_exchanged(flat):
+            return flat.rearrange("p (n c) -> p n c", c=2)[:, :, ::-1]
+
+        def transpose_tables():
+            flipped = flip_banks.tile([P, 4, P], BF16)
+            for i, table in enumerate((cos_sb, sin_exchanged)):
+                for j in range(2):
+                    nc.tensor.transpose(
+                        out=flipped[:, 2 * i + j, :],
+                        in_=table[:, j * HEAD_DIM : (j + 1) * HEAD_DIM],
+                        identity=identity_bf16[:],
+                    )
+            nc.scalar.copy(
+                out=tables_t[:].rearrange("p i t -> p (i t)"),
+                in_=flipped[:].rearrange("p n t -> p (n t)"),
+            )
+
+        def multiply_t(h):
+            i = SLAB_OF_HEAD[h]
+            column = (h - SLABS[i][0]) * HEAD_DIM
+            head = slice(column, column + HEAD_DIM)
+            bank = product_banks.tile([P, T], F32)
+            nc.tensor.matmul_mx(
+                out=bank[:],
+                lhsT=codes_w[i][:, head].bitcast(FP8X4),
+                lhsT_scale=scales_w[i][:, head],
+                rhs=x_codes[:].bitcast(FP8X4),
+                rhs_scale=x_scales[:],
+                start=True,
+                stop=True,
+            )
+            banks[h] = bank
+
+        def part_t(h, i):
+            nc.vector.tensor_tensor(
+                out=new_part(h, ("cos", "sin")[i])[:],
+                in0=banks[h][:],
+                in1=tables_t[:, i, :],
+                op=MULT,
+            )
+
+        def add_and_store_t(h):
+            flipped = flip_banks.tile([P, 2, HEAD_DIM], F32)
+            for j in range(2):
+                for i, order in enumerate((identity, exchange)):
+                    nc.tensor.matmul(
+                        out=flipped[:, j, :],
+                        lhsT=parts_of[h][i][:, j * P : (j + 1) * P],
+                        rhs=order[:],
+                        is_transpose=True,
+                        start=i == 0,
+                        stop=i == 1,
+                    )
+            total = rotated.tile([P, 2 * HEAD_DIM], F32)
+            nc.scalar.mul(
+                out=total[:],
+                in_=flipped[:].rearrange("p j d -> p (j d)"),
+                mul=(1.0, SCALING)[h // HEADS],
+            )
+            out = (out_0, out_1)[h // HEADS].rearrange("b h (p j) d -> p (b h) (j d)", j=2)
+            nc.sync.dma_start(out=out[:, h % HEADS, :], in_=total[:])
+
         with tc.manual_schedule():
             zeros = keep.tile([P, P], F32)
             nc.vector.memset(zeros[:], 0.0)
+            nc.scalar.copy(out=identity_bf16[:], in_=identity[:])
+            nc.scalar.copy(
+                out=exchange[:].rearrange("p (n c) -> p n c", c=2),
+                in_=pairs_exchanged(identity[:]),
+            )
             keep_tensor_busy(zeros[:].bitcast(BF16), 128)
             keep_tensor_busy(zeros[:], 416)
             transpose_weights(0)
@@ -197,21 +281,41 @@ def tile_nucleusxmultiscaleretention_pa_s_kernel(
             transpose_weights(1)
             group_weights(1)
             negate_even_sines()
+            nc.gpsimd.tensor_copy(
+                out=sin_exchanged[:].rearrange("p (n c) -> p n c", c=2),
+                in_=pairs_exchanged(sin_sb[:]),
+            )
             transpose_weights(2)
             group_weights(2)
             quantise_positions()
             quantise_weights(1)
             multiply(0)
-            for h in range(last + 1):
+            for h in range(4):
                 if h + 3 < len(SLABS):
                     transpose_weights(h + 3)
                     group_weights(h + 3)
-                if h < last:
+                if h < 3:
                     multiply(h + 1)
-                rotate(h)
-                if h < last - 1:
+                cosine(h)
+                sine(h)
+                if h < 3:
                     add_and_store(h, nc.gpsimd)
                 if h + 2 < len(SLABS):
                     quantise_weights(h + 2)
-            for h in (last - 1, last):
-                add_and_store(h, nc.vector)
+            transpose_tables()
+            for h in TENSOR_ADDS:
+                multiply_t(h)
+            multiply(7)
+            for h in GPSIMD_COSINES:
+                cosine_on_gpsimd(h)
+            add_and_store(3, nc.gpsimd)
+            for h in TENSOR_ADDS:
+                if h not in GPSIMD_COSINES:
+                    part_t(h, 0)
+                part_t(h, 1)
+                if h != TENSOR_ADDS[-1]:
+                    add_and_store_t(h)
+            cosine(7)
+            sine(7)
+            add_and_store(7, nc.vector)
+            add_and_store_t(TENSOR_ADDS[-1])

@@ -281,9 +281,13 @@ def tile_nucleusxmultiscaleretention_pa_s_kernel(
             transpose_weights(1)
             group_weights(1)
             negate_even_sines()
-            nc.gpsimd.tensor_copy(
+            nc.gpsimd.tensor_scalar(
                 out=sin_exchanged[:].rearrange("p (n c) -> p n c", c=2),
-                in_=pairs_exchanged(sin_sb[:]),
+                in0=pairs_exchanged(sin_sb[:]),
+                scalar1=1.0,
+                scalar2=0.0,
+                op0=MULT,
+                op1=ADD,
             )
             transpose_weights(2)
             group_weights(2)

@@ -19,8 +19,7 @@ HEAD_DIM = 128
 SCALING = HEAD_DIM**-0.5
 SLABS = ((0, 1), (1, 1), (2, 2), (4, 2), (6, 2))
 SLAB_OF_HEAD = [i for i, (first, n) in enumerate(SLABS) for h in range(n)]
-TENSOR_ADDS = (4, 5, 6)
-GPSIMD_COSINES = (5,)
+TENSOR_ADDS = (4, 5)
 FLOPS = 2 * T * E * (2 * E)
 
 
@@ -165,13 +164,6 @@ def tile_nucleusxmultiscaleretention_pa_s_kernel(
                 op1=MULT,
             )
 
-        def cosine_on_gpsimd(h):
-            copied = rotated.tile([P, T], F32)
-            nc.scalar.copy(out=copied[:], in_=banks[h][:])
-            nc.gpsimd.tensor_tensor(
-                out=new_part(h, "cos")[:], in0=copied[:], in1=tables_t[:, 0, :], op=MULT
-            )
-
         def cosine(h):
             straight = banks[h][:].rearrange("p (n c) -> p n c", c=2)
             rotate(h, (new_part(h, "cos"), straight, cos_sb))
@@ -302,24 +294,20 @@ def tile_nucleusxmultiscaleretention_pa_s_kernel(
                     multiply(h + 1)
                 cosine(h)
                 sine(h)
-                if h < 3:
-                    add_and_store(h, nc.gpsimd)
+                add_and_store(h, nc.gpsimd)
                 if h + 2 < len(SLABS):
                     quantise_weights(h + 2)
             transpose_tables()
             for h in TENSOR_ADDS:
                 multiply_t(h)
+            multiply(6)
             multiply(7)
-            for h in GPSIMD_COSINES:
-                cosine_on_gpsimd(h)
-            add_and_store(3, nc.gpsimd)
             for h in TENSOR_ADDS:
-                if h not in GPSIMD_COSINES:
-                    part_t(h, 0)
+                part_t(h, 0)
                 part_t(h, 1)
-                if h != TENSOR_ADDS[-1]:
-                    add_and_store_t(h)
-            cosine(7)
-            sine(7)
-            add_and_store(7, nc.vector)
-            add_and_store_t(TENSOR_ADDS[-1])
+                add_and_store_t(h)
+            for h in (6, 7):
+                cosine(h)
+                sine(h)
+            for h in (6, 7):
+                add_and_store(h, nc.vector)

@@ -19,7 +19,6 @@ HEAD_DIM = 128
 SCALING = HEAD_DIM**-0.5
 SLABS = ((0, 1), (1, 1), (2, 2), (4, 2), (6, 2))
 SLAB_OF_HEAD = [i for i, (first, n) in enumerate(SLABS) for h in range(n)]
-TENSOR_ADDS = (4, 5)
 FLOPS = 2 * T * E * (2 * E)
 
 
@@ -48,24 +47,23 @@ def tile_nucleusxmultiscaleretention_pa_s_kernel(
             nc.sync.dma_start(out=raw[:], in_=rows)
             return raw
 
-        def load_table(label, table):
-            loaded = keep.tile([P, 2 * HEAD_DIM], BF16, name=label)
-            nc.sync.dma_start(out=loaded[:], in_=table.rearrange("(p j) d -> p (j d)", j=2))
-            return loaded
+        tables = keep.tile([P, 2, 2 * HEAD_DIM], BF16)
+        sin_sb = keep.tile([P, 2 * HEAD_DIM], BF16)
 
         raw_w = [load_weights(0)]
         raw_x = [load_positions(0), load_positions(1)]
         raw_w.extend([load_weights(1), load_weights(2)])
-        cos_sb = load_table("cos_sb", cos)
-        sin_sb = load_table("sin_sb", sin)
+        nc.sync.dma_start(out=sin_sb[:], in_=sin.rearrange("(p j) d -> p (j d)", j=2))
+        nc.sync.dma_start(out=tables[:, 0, :], in_=cos.rearrange("(p j) d -> p (j d)", j=2))
         raw_w.extend([load_weights(i) for i in range(3, len(SLABS))])
 
+        zeros = keep.tile([P, 1], F32)
+        nc.gpsimd.memset(zeros[:], 0.0)
+        signs = keep.tile([P, 2 * HEAD_DIM], BF16)
+        nc.vector.memset(signs[:], 1.0)
+        nc.vector.memset(signs[:].rearrange("p (n c) -> p n c", c=2)[:, :, 1:2], -1.0)
         identity = keep.tile([P, P], F32)
         make_identity(nc, identity[:])
-
-        def negate_even_sines():
-            sin_even = sin_sb[:].rearrange("p (n c) -> p n c", c=2)[:, :, 0:1]
-            nc.scalar.mul(out=sin_even, in_=sin_even, mul=-1.0)
 
         def transpose_rows(raw, out):
             words = raw.bitcast(F32)
@@ -85,7 +83,7 @@ def tile_nucleusxmultiscaleretention_pa_s_kernel(
                 flipped = flip_banks.tile([P, 2, P], F32)
                 transpose_rows(raw_x[j][:], flipped[:])
                 grouped = keep.tile([P, 2 * P], F32, name="x_grouped%d" % j, align_bytes=64)
-                copy = nc.scalar.copy if j == 0 else nc.vector.tensor_copy
+                copy = nc.scalar.copy
                 copy(
                     out=grouped[:].rearrange("p (r u) -> p r u", u=2),
                     in_=flipped[:].rearrange("p u r -> p r u"),
@@ -130,59 +128,149 @@ def tile_nucleusxmultiscaleretention_pa_s_kernel(
             )
             codes_w[i], scales_w[i] = codes, scales
 
-        def multiply(h):
+        def weights_of(h):
             i = SLAB_OF_HEAD[h]
             column = (h - SLABS[i][0]) * HEAD_DIM
             head = slice(column, column + HEAD_DIM)
-            bank = product_banks.tile([P, 2 * HEAD_DIM], F32)
+            return codes_w[i][:, head].bitcast(FP8X4), scales_w[i][:, head]
+
+        def new_bank(h):
+            if h not in banks:
+                bank = product_banks.tile([P, T], F32)
+                banks[h] = bank
+            return banks[h]
+
+        def fill(h, n, columns=256):
+            fill_bank(new_bank(h)[:], n, columns)
+
+        def fill_bank(bank, n, columns=256):
+            codes, scales = weights_of(0)
+            for i in range(n):
+                nc.tensor.matmul_mx(
+                    out=bank[:, 0:columns],
+                    lhsT=codes,
+                    lhsT_scale=scales,
+                    rhs=x_codes[:, 0:columns].bitcast(FP8X4),
+                    rhs_scale=x_scales[:, 0:columns],
+                    start=True,
+                    stop=True,
+                )
+
+        def multiply_half(h, j):
+            codes, scales = weights_of(h)
+            bank = product_banks.tile([P, HEAD_DIM], F32, name="bank")
+            half = slice(j * P, (j + 1) * P)
+            nc.tensor.matmul_mx(
+                out=bank[:],
+                lhsT=x_codes[:, half].bitcast(FP8X4),
+                lhsT_scale=x_scales[:, half],
+                rhs=codes,
+                rhs_scale=scales,
+                start=True,
+                stop=True,
+            )
+            banks[h, j] = bank
+
+        def rotate_half(h, j):
+            if j == 0:
+                parts_of[h] = rotated.tile([P, 2, T], F32, name="parts")
+            half = slice(j * HEAD_DIM, (j + 1) * HEAD_DIM)
+            nc.vector.scalar_tensor_tensor(
+                out=parts_of[h][:, :, half],
+                in0=banks[h, j][:].unsqueeze(1).to_broadcast([P, 2, HEAD_DIM]),
+                scalar=(1.0, SCALING)[h // HEADS],
+                in1=tables[:, :, half],
+                op0=MULT,
+                op1=MULT,
+            )
+
+        def multiply(h):
+            codes, scales = weights_of(h)
+            bank = new_bank(h)
             for j in range(2):
                 half = slice(j * P, (j + 1) * P)
                 nc.tensor.matmul_mx(
                     out=bank[:, half],
                     lhsT=x_codes[:, half].bitcast(FP8X4),
                     lhsT_scale=x_scales[:, half],
-                    rhs=codes_w[i][:, head].bitcast(FP8X4),
-                    rhs_scale=scales_w[i][:, head],
+                    rhs=codes,
+                    rhs_scale=scales,
                     start=True,
                     stop=True,
                 )
-            banks[h] = bank
 
-        def new_part(h, label):
-            part = rotated.tile([P, 2 * HEAD_DIM], F32, name=label + "_part")
-            parts_of.setdefault(h, []).append(part)
-            return part
+        def multiply_t(h):
+            codes, scales = weights_of(h)
+            bank = new_bank(h)
+            nc.tensor.matmul_mx(
+                out=bank[:],
+                lhsT=codes,
+                lhsT_scale=scales,
+                rhs=x_codes[:].bitcast(FP8X4),
+                rhs_scale=x_scales[:],
+                start=True,
+                stop=True,
+            )
 
-        def rotate(h, part_read_table):
-            part, read, table = part_read_table
+        def rotate(h, pair_of_tables):
+            parts = rotated.tile([P, 2, T], F32)
             nc.vector.scalar_tensor_tensor(
-                out=part[:].rearrange("p (n c) -> p n c", c=2),
-                in0=read,
+                out=parts[:],
+                in0=banks[h][:].unsqueeze(1).to_broadcast([P, 2, T]),
                 scalar=(1.0, SCALING)[h // HEADS],
-                in1=table[:].rearrange("p (n c) -> p n c", c=2),
+                in1=pair_of_tables[:],
+                op0=MULT,
+                op1=MULT,
+            )
+            parts_of[h] = parts
+
+        def rotate_one(h, pair_of_tables, i):
+            if i == 0:
+                parts_of[h] = rotated.tile([P, 2, T], F32, name="parts")
+            nc.vector.scalar_tensor_tensor(
+                out=parts_of[h][:, i, :],
+                in0=banks[h][:],
+                scalar=(1.0, SCALING)[h // HEADS],
+                in1=pair_of_tables[:, i, :],
                 op0=MULT,
                 op1=MULT,
             )
 
-        def cosine(h):
-            straight = banks[h][:].rearrange("p (n c) -> p n c", c=2)
-            rotate(h, (new_part(h, "cos"), straight, cos_sb))
+        def pairs_exchanged(flat):
+            return flat.rearrange("p (n c) -> p n c", c=2)[:, :, ::-1]
 
-        def sine(h):
-            crossed = banks[h][:].rearrange("p (n c) -> p n c", c=2)[:, :, ::-1]
-            rotate(h, (new_part(h, "sin"), crossed, sin_sb))
+        def store(h, total):
+            out = (out_0, out_1)[h // HEADS].rearrange("b h (p j) d -> p (b h) (j d)", j=2)
+            nc.sync.dma_start(out=out[:, h % HEADS, :], in_=total)
 
         def add_and_store(h, adder):
-            cos_part, sin_part = parts_of[h]
-            adder.tensor_tensor(out=cos_part[:], in0=cos_part[:], in1=sin_part[:], op=ADD)
-            out = (out_0, out_1)[h // HEADS].rearrange("b h (p j) d -> p (b h) (j d)", j=2)
-            nc.sync.dma_start(out=out[:, h % HEADS, :], in_=cos_part[:])
+            parts = parts_of[h]
+            adder.tensor_tensor(
+                out=parts[:, 0, :].rearrange("p (n c) -> p n c", c=2),
+                in0=parts[:, 0, :].rearrange("p (n c) -> p n c", c=2),
+                in1=pairs_exchanged(parts[:, 1, :]),
+                op=ADD,
+            )
+            store(h, parts[:, 0, :])
+
+        products = {}
+
+        def copy_product(h):
+            product = rotated.tile([P, 2 * HEAD_DIM], F32)
+            nc.scalar.mul(out=product[:], in_=banks[h][:], mul=(1.0, SCALING)[h // HEADS])
+            products[h] = product
+
+        def cosine_gpsimd(h, pair_of_tables):
+            parts_of[h] = rotated.tile([P, 2, T], F32, name="parts")
+            nc.gpsimd.tensor_tensor(
+                out=parts_of[h][:, 0, :], in0=products[h][:], in1=pair_of_tables[:, 0, :], op=MULT
+            )
 
         def keep_tensor_busy(operand, columns):
             bank = product_banks.tile([P, columns], F32)
             nc.tensor.matmul(
                 out=bank[:],
-                lhsT=operand[:, 0:P],
+                lhsT=operand[:, 0:1].to_broadcast([P, P]),
                 rhs=operand[:, 0:1].to_broadcast([P, columns]),
                 start=True,
                 stop=True,
@@ -190,81 +278,66 @@ def tile_nucleusxmultiscaleretention_pa_s_kernel(
 
         exchange = keep.tile([P, P], F32)
         identity_bf16 = keep.tile([P, P], BF16)
-        sin_exchanged = keep.tile([P, 2 * HEAD_DIM], BF16)
         tables_t = keep.tile([P, 2, T], BF16)
 
-        def pairs_exchanged(flat):
-            return flat.rearrange("p (n c) -> p n c", c=2)[:, :, ::-1]
+        def exchange_sines():
+            nc.vector.tensor_tensor(
+                out=tables[:, 1, :].rearrange("p (n c) -> p n c", c=2),
+                in0=pairs_exchanged(sin_sb[:]),
+                in1=signs[:].rearrange("p (n c) -> p n c", c=2),
+                op=MULT,
+            )
 
         def transpose_tables():
             flipped = flip_banks.tile([P, 4, P], BF16)
-            for i, table in enumerate((cos_sb, sin_exchanged)):
+            for i in range(2):
                 for j in range(2):
                     nc.tensor.transpose(
                         out=flipped[:, 2 * i + j, :],
-                        in_=table[:, j * HEAD_DIM : (j + 1) * HEAD_DIM],
+                        in_=tables[:, i, j * HEAD_DIM : (j + 1) * HEAD_DIM],
                         identity=identity_bf16[:],
                     )
+            return flipped
+
+        def copy_tables(flipped):
             nc.scalar.copy(
                 out=tables_t[:].rearrange("p i t -> p (i t)"),
                 in_=flipped[:].rearrange("p n t -> p (n t)"),
             )
 
-        def multiply_t(h):
-            i = SLAB_OF_HEAD[h]
-            column = (h - SLABS[i][0]) * HEAD_DIM
-            head = slice(column, column + HEAD_DIM)
-            bank = product_banks.tile([P, T], F32)
-            nc.tensor.matmul_mx(
-                out=bank[:],
-                lhsT=codes_w[i][:, head].bitcast(FP8X4),
-                lhsT_scale=scales_w[i][:, head],
-                rhs=x_codes[:].bitcast(FP8X4),
-                rhs_scale=x_scales[:],
-                start=True,
-                stop=True,
-            )
-            banks[h] = bank
+        totals = {}
 
-        def part_t(h, i):
-            nc.vector.tensor_tensor(
-                out=new_part(h, ("cos", "sin")[i])[:],
-                in0=banks[h][:],
-                in1=tables_t[:, i, :],
-                op=MULT,
-            )
-
-        def add_and_store_t(h):
+        def add_t(h, n=0):
             flipped = flip_banks.tile([P, 2, HEAD_DIM], F32)
+            fill_bank(flipped[:].rearrange("p j d -> p (j d)"), n)
             for j in range(2):
                 for i, order in enumerate((identity, exchange)):
                     nc.tensor.matmul(
                         out=flipped[:, j, :],
-                        lhsT=parts_of[h][i][:, j * P : (j + 1) * P],
+                        lhsT=parts_of[h][:, i, j * P : (j + 1) * P],
                         rhs=order[:],
                         is_transpose=True,
                         start=i == 0,
                         stop=i == 1,
                     )
+            totals[h] = flipped
+
+        def store_t(h):
             total = rotated.tile([P, 2 * HEAD_DIM], F32)
-            nc.scalar.mul(
+            nc.scalar.copy(
                 out=total[:],
-                in_=flipped[:].rearrange("p j d -> p (j d)"),
-                mul=(1.0, SCALING)[h // HEADS],
+                in_=totals[h][:].rearrange("p j d -> p (j d)"),
             )
-            out = (out_0, out_1)[h // HEADS].rearrange("b h (p j) d -> p (b h) (j d)", j=2)
-            nc.sync.dma_start(out=out[:, h % HEADS, :], in_=total[:])
+            store(h, total[:])
 
         with tc.manual_schedule():
-            zeros = keep.tile([P, P], F32)
-            nc.vector.memset(zeros[:], 0.0)
             nc.scalar.copy(out=identity_bf16[:], in_=identity[:])
             nc.scalar.copy(
                 out=exchange[:].rearrange("p (n c) -> p n c", c=2),
                 in_=pairs_exchanged(identity[:]),
             )
-            keep_tensor_busy(zeros[:].bitcast(BF16), 128)
-            keep_tensor_busy(zeros[:], 416)
+            keep_tensor_busy(zeros[:].bitcast(BF16), 40)
+            keep_tensor_busy(zeros[:], 512)
             transpose_weights(0)
             group_weights(0)
             quantise_weights(0)
@@ -272,42 +345,48 @@ def tile_nucleusxmultiscaleretention_pa_s_kernel(
             keep_tensor_busy(zeros[:], 256)
             transpose_weights(1)
             group_weights(1)
-            negate_even_sines()
-            nc.gpsimd.tensor_scalar(
-                out=sin_exchanged[:].rearrange("p (n c) -> p n c", c=2),
-                in0=pairs_exchanged(sin_sb[:]),
-                scalar1=1.0,
-                scalar2=0.0,
-                op0=MULT,
-                op1=ADD,
-            )
+            quantise_positions()
+            exchange_sines()
             transpose_weights(2)
             group_weights(2)
-            quantise_positions()
             quantise_weights(1)
             multiply(0)
-            for h in range(4):
-                if h + 3 < len(SLABS):
-                    transpose_weights(h + 3)
-                    group_weights(h + 3)
-                if h < 3:
-                    multiply(h + 1)
-                cosine(h)
-                sine(h)
-                add_and_store(h, nc.gpsimd)
-                if h + 2 < len(SLABS):
-                    quantise_weights(h + 2)
-            transpose_tables()
-            for h in TENSOR_ADDS:
-                multiply_t(h)
+            flipped_tables = transpose_tables()
+            copy_tables(flipped_tables)
+            transpose_weights(3)
+            group_weights(3)
+            multiply(1)
+            rotate(0, tables)
+            add_and_store(0, nc.gpsimd)
+            quantise_weights(2)
+            transpose_weights(4)
+            group_weights(4)
+            multiply_t(2)
+            multiply_t(3)
+            fill(4, 2)
+            rotate(1, tables)
+            add_and_store(1, nc.gpsimd)
+            quantise_weights(3)
+            rotate(2, tables_t)
+            multiply_t(4)
+            multiply(5)
+            copy_product(4)
+            cosine_gpsimd(4, tables_t)
+            fill(6, 1)
+            add_t(2)
+            store_t(2)
+            rotate(3, tables_t)
+            quantise_weights(4)
+            add_t(3)
+            store_t(3)
             multiply(6)
             multiply(7)
-            for h in TENSOR_ADDS:
-                part_t(h, 0)
-                part_t(h, 1)
-                add_and_store_t(h)
-            for h in (6, 7):
-                cosine(h)
-                sine(h)
-            for h in (6, 7):
-                add_and_store(h, nc.vector)
+            rotate(5, tables)
+            add_and_store(5, nc.gpsimd)
+            rotate_one(4, tables_t, 1)
+            add_t(4)
+            store_t(4)
+            rotate(6, tables)
+            add_and_store(6, nc.gpsimd)
+            rotate(7, tables)
+            add_and_store(7, nc.vector)

@@ -387,6 +387,6 @@ def tile_nucleusxmultiscaleretention_pa_s_kernel(
             add_t(4)
             store_t(4)
             rotate(6, tables)
-            add_and_store(6, nc.gpsimd)
             rotate(7, tables)
+            add_and_store(6, nc.vector)
             add_and_store(7, nc.vector)

@@ -58,7 +58,7 @@ def tile_nucleusxmultiscaleretention_pa_s_kernel(
         raw_w.extend([load_weights(i) for i in range(3, len(SLABS))])
 
         zeros = keep.tile([P, 1], F32)
-        nc.gpsimd.memset(zeros[:], 0.0)
+        nc.vector.memset(zeros[:], 0.0)
         signs = keep.tile([P, 2 * HEAD_DIM], BF16)
         nc.vector.memset(signs[:], 1.0)
         nc.vector.memset(signs[:].rearrange("p (n c) -> p n c", c=2)[:, :, 1:2], -1.0)
@@ -83,7 +83,7 @@ def tile_nucleusxmultiscaleretention_pa_s_kernel(
                 flipped = flip_banks.tile([P, 2, P], F32)
                 transpose_rows(raw_x[j][:], flipped[:])
                 grouped = keep.tile([P, 2 * P], F32, name="x_grouped%d" % j, align_bytes=64)
-                copy = nc.scalar.copy
+                copy = nc.vector.tensor_copy if j == 0 else nc.scalar.copy
                 copy(
                     out=grouped[:].rearrange("p (r u) -> p r u", u=2),
                     in_=flipped[:].rearrange("p u r -> p r u"),
@@ -340,8 +340,8 @@ def tile_nucleusxmultiscaleretention_pa_s_kernel(
             keep_tensor_busy(zeros[:], 512)
             transpose_weights(0)
             group_weights(0)
-            quantise_weights(0)
             transpose_positions()
+            quantise_weights(0)
             keep_tensor_busy(zeros[:], 256)
             transpose_weights(1)
             group_weights(1)

from contextlib import ExitStack

import concourse.mybir as mybir
from concourse.masks import make_identity

BF16 = mybir.dt.bfloat16
F32 = mybir.dt.float32
U32 = mybir.dt.uint32
U8 = mybir.dt.uint8
FP8X4 = mybir.dt.float8_e4m3fn_x4
MULT = mybir.AluOpType.mult
ADD = mybir.AluOpType.add

P = 128
T = 256
E = 512
HEADS = 4
HEAD_DIM = 128
SCALING = HEAD_DIM**-0.5
SLABS = ((0, 1), (1, 1), (2, 2), (4, 2), (6, 2))
SLAB_OF_HEAD = [i for i, (first, n) in enumerate(SLABS) for h in range(n)]
FLOPS = 2 * T * E * (2 * E)


def tile_nucleusxmultiscaleretention_pa_s_kernel(
    tc, hidden_states, wq, wk, sin, cos, out_0, out_1
):
    nc = tc.nc
    with ExitStack() as ctx:
        keep = ctx.enter_context(tc.tile_pool(name="keep", bufs=1))
        stage = ctx.enter_context(tc.tile_pool(name="stage", bufs=3))
        rotated = ctx.enter_context(tc.tile_pool(name="rotated", bufs=2 * HEADS))
        flip_banks = ctx.enter_context(tc.psum_pool(name="flip_banks", bufs=4))
        product_banks = ctx.enter_context(tc.psum_pool(name="product_banks", bufs=4))

        def load_weights(i):
            first, n = SLABS[i]
            row = first % HEADS * HEAD_DIM
            rows = (wq, wk)[first // HEADS][row : row + n * HEAD_DIM, :]
            raw = keep.tile([P, n * E], BF16, name="raw_w%d" % i)
            nc.sync.dma_start(out=raw[:], in_=rows.rearrange("(p j) k -> p (j k)", j=n))
            return raw

        def load_positions(j):
            rows = hidden_states.flatten_outer_dims().rearrange("(p j) k -> j p k", j=2)[j]
            raw = keep.tile([P, E], BF16, name="raw_x%d" % j)
            nc.sync.dma_start(out=raw[:], in_=rows)
            return raw

        tables = keep.tile([P, 2, 2 * HEAD_DIM], BF16)
        sin_sb = keep.tile([P, 2 * HEAD_DIM], BF16)

        raw_w = [load_weights(0)]
        raw_x = [load_positions(0), load_positions(1)]
        raw_w.extend([load_weights(1), load_weights(2)])
        nc.sync.dma_start(out=sin_sb[:], in_=sin.rearrange("(p j) d -> p (j d)", j=2))
        nc.sync.dma_start(out=tables[:, 0, :], in_=cos.rearrange("(p j) d -> p (j d)", j=2))
        raw_w.extend([load_weights(i) for i in range(3, len(SLABS))])

        zeros = keep.tile([P, 1], F32)
        nc.vector.memset(zeros[:], 0.0)
        signs = keep.tile([P, 2 * HEAD_DIM], BF16)
        nc.vector.memset(signs[:], 1.0)
        nc.vector.memset(signs[:].rearrange("p (n c) -> p n c", c=2)[:, :, 1:2], -1.0)
        identity = keep.tile([P, P], F32)
        make_identity(nc, identity[:])

        def transpose_rows(raw, out):
            words = raw.bitcast(F32)
            for u in range(2):
                nc.tensor.transpose(
                    out=out[:, u, :],
                    in_=words[:, u * P : (u + 1) * P],
                    identity=identity[:],
                )

        x_codes = keep.tile([P, T], U32, align_bytes=64)
        x_scales = keep.tile([P, T], U8, align_bytes=64)
        x_grouped = []

        def transpose_positions():
            for j in range(2):
                flipped = flip_banks.tile([P, 2, P], F32)
                transpose_rows(raw_x[j][:], flipped[:])
                grouped = keep.tile([P, 2 * P], F32, name="x_grouped%d" % j, align_bytes=64)
                copy = nc.vector.tensor_copy if j == 0 else nc.scalar.copy
                copy(
                    out=grouped[:].rearrange("p (r u) -> p r u", u=2),
                    in_=flipped[:].rearrange("p u r -> p r u"),
                )
                x_grouped.append(grouped)

        def quantise_positions():
            for j in range(2):
                half = slice(j * P, (j + 1) * P)
                nc.vector.quantize_mx(
                    out=x_codes[:, half].bitcast(FP8X4),
                    scales=x_scales[:, half],
                    in_=x_grouped[j][:].bitcast(BF16),
                )

        flipped_w, grouped_w, codes_w, scales_w, banks, parts_of = {}, {}, {}, {}, {}, {}

        def transpose_weights(i):
            n = SLABS[i][1]
            flipped = flip_banks.tile([P, 2, n * P], F32)
            for j in range(n):
                transpose_rows(
                    raw_w[i][:, j * E : (j + 1) * E], flipped[:, :, j * P : (j + 1) * P]
                )
            flipped_w[i] = flipped

        def group_weights(i):
            n = SLABS[i][1]
            grouped = stage.tile([P, 2 * n * P], F32, align_bytes=64)
            nc.scalar.copy(
                out=grouped[:].rearrange("p (r j u) -> p r j u", j=n, u=2),
                in_=flipped_w[i][:].rearrange("p u (j r) -> p r j u", j=n),
            )
            grouped_w[i] = grouped

        def quantise_weights(i):
            n = SLABS[i][1]
            codes = keep.tile([P, n * P], U32, name="w_codes%d" % i, align_bytes=64)
            scales = keep.tile([P, n * P], U8, name="w_scales%d" % i, align_bytes=64)
            nc.vector.quantize_mx(
                out=codes[:].bitcast(FP8X4), scales=scales[:], in_=grouped_w[i][:].bitcast(BF16)
            )
            codes_w[i], scales_w[i] = codes, scales

        def weights_of(h):
            i = SLAB_OF_HEAD[h]
            column = (h - SLABS[i][0]) * HEAD_DIM
            head = slice(column, column + HEAD_DIM)
            return codes_w[i][:, head].bitcast(FP8X4), scales_w[i][:, head]

        def new_bank(h):
            if h not in banks:
                bank = product_banks.tile([P, T], F32)
                banks[h] = bank
            return banks[h]

        def fill(h, n, columns=256):
            fill_bank(new_bank(h)[:], n, columns)

        def fill_bank(bank, n, columns=256):
            codes, scales = weights_of(0)
            for i in range(n):
                nc.tensor.matmul_mx(
                    out=bank[:, 0:columns],
                    lhsT=codes,
                    lhsT_scale=scales,
                    rhs=x_codes[:, 0:columns].bitcast(FP8X4),
                    rhs_scale=x_scales[:, 0:columns],
                    start=True,
                    stop=True,
                )

        def multiply_half(h, j):
            codes, scales = weights_of(h)
            bank = product_banks.tile([P, HEAD_DIM], F32, name="bank")
            half = slice(j * P, (j + 1) * P)
            nc.tensor.matmul_mx(
                out=bank[:],
                lhsT=x_codes[:, half].bitcast(FP8X4),
                lhsT_scale=x_scales[:, half],
                rhs=codes,
                rhs_scale=scales,
                start=True,
                stop=True,
            )
            banks[h, j] = bank

        def rotate_half(h, j):
            if j == 0:
                parts_of[h] = rotated.tile([P, 2, T], F32, name="parts")
            half = slice(j * HEAD_DIM, (j + 1) * HEAD_DIM)
            nc.vector.scalar_tensor_tensor(
                out=parts_of[h][:, :, half],
                in0=banks[h, j][:].unsqueeze(1).to_broadcast([P, 2, HEAD_DIM]),
                scalar=(1.0, SCALING)[h // HEADS],
                in1=tables[:, :, half],
                op0=MULT,
                op1=MULT,
            )

        def multiply(h):
            codes, scales = weights_of(h)
            bank = new_bank(h)
            for j in range(2):
                half = slice(j * P, (j + 1) * P)
                nc.tensor.matmul_mx(
                    out=bank[:, half],
                    lhsT=x_codes[:, half].bitcast(FP8X4),
                    lhsT_scale=x_scales[:, half],
                    rhs=codes,
                    rhs_scale=scales,
                    start=True,
                    stop=True,
                )

        def multiply_t(h):
            codes, scales = weights_of(h)
            bank = new_bank(h)
            nc.tensor.matmul_mx(
                out=bank[:],
                lhsT=codes,
                lhsT_scale=scales,
                rhs=x_codes[:].bitcast(FP8X4),
                rhs_scale=x_scales[:],
                start=True,
                stop=True,
            )

        def rotate(h, pair_of_tables):
            parts = rotated.tile([P, 2, T], F32)
            nc.vector.scalar_tensor_tensor(
                out=parts[:],
                in0=banks[h][:].unsqueeze(1).to_broadcast([P, 2, T]),
                scalar=(1.0, SCALING)[h // HEADS],
                in1=pair_of_tables[:],
                op0=MULT,
                op1=MULT,
            )
            parts_of[h] = parts

        def rotate_one(h, pair_of_tables, i):
            if i == 0:
                parts_of[h] = rotated.tile([P, 2, T], F32, name="parts")
            nc.vector.scalar_tensor_tensor(
                out=parts_of[h][:, i, :],
                in0=banks[h][:],
                scalar=(1.0, SCALING)[h // HEADS],
                in1=pair_of_tables[:, i, :],
                op0=MULT,
                op1=MULT,
            )

        def pairs_exchanged(flat):
            return flat.rearrange("p (n c) -> p n c", c=2)[:, :, ::-1]

        def store(h, total):
            out = (out_0, out_1)[h // HEADS].rearrange("b h (p j) d -> p (b h) (j d)", j=2)
            nc.sync.dma_start(out=out[:, h % HEADS, :], in_=total)

        def add_and_store(h, adder):
            parts = parts_of[h]
            adder.tensor_tensor(
                out=parts[:, 0, :].rearrange("p (n c) -> p n c", c=2),
                in0=parts[:, 0, :].rearrange("p (n c) -> p n c", c=2),
                in1=pairs_exchanged(parts[:, 1, :]),
                op=ADD,
            )
            store(h, parts[:, 0, :])

        products = {}

        def copy_product(h):
            product = rotated.tile([P, 2 * HEAD_DIM], F32)
            nc.scalar.mul(out=product[:], in_=banks[h][:], mul=(1.0, SCALING)[h // HEADS])
            products[h] = product

        def cosine_gpsimd(h, pair_of_tables):
            parts_of[h] = rotated.tile([P, 2, T], F32, name="parts")
            nc.gpsimd.tensor_tensor(
                out=parts_of[h][:, 0, :], in0=products[h][:], in1=pair_of_tables[:, 0, :], op=MULT
            )

        def keep_tensor_busy(operand, columns):
            bank = product_banks.tile([P, columns], F32)
            nc.tensor.matmul(
                out=bank[:],
                lhsT=operand[:, 0:1].to_broadcast([P, P]),
                rhs=operand[:, 0:1].to_broadcast([P, columns]),
                start=True,
                stop=True,
            )

        exchange = keep.tile([P, P], F32)
        identity_bf16 = keep.tile([P, P], BF16)
        tables_t = keep.tile([P, 2, T], BF16)

        def exchange_sines():
            nc.vector.tensor_tensor(
                out=tables[:, 1, :].rearrange("p (n c) -> p n c", c=2),
                in0=pairs_exchanged(sin_sb[:]),
                in1=signs[:].rearrange("p (n c) -> p n c", c=2),
                op=MULT,
            )

        def transpose_tables():
            flipped = flip_banks.tile([P, 4, P], BF16)
            for i in range(2):
                for j in range(2):
                    nc.tensor.transpose(
                        out=flipped[:, 2 * i + j, :],
                        in_=tables[:, i, j * HEAD_DIM : (j + 1) * HEAD_DIM],
                        identity=identity_bf16[:],
                    )
            return flipped

        def copy_tables(flipped):
            nc.scalar.copy(
                out=tables_t[:].rearrange("p i t -> p (i t)"),
                in_=flipped[:].rearrange("p n t -> p (n t)"),
            )

        totals = {}

        def add_t(h, n=0):
            flipped = flip_banks.tile([P, 2, HEAD_DIM], F32)
            fill_bank(flipped[:].rearrange("p j d -> p (j d)"), n)
            for j in range(2):
                for i, order in enumerate((identity, exchange)):
                    nc.tensor.matmul(
                        out=flipped[:, j, :],
                        lhsT=parts_of[h][:, i, j * P : (j + 1) * P],
                        rhs=order[:],
                        is_transpose=True,
                        start=i == 0,
                        stop=i == 1,
                    )
            totals[h] = flipped

        def store_t(h):
            total = rotated.tile([P, 2 * HEAD_DIM], F32)
            nc.scalar.copy(
                out=total[:],
                in_=totals[h][:].rearrange("p j d -> p (j d)"),
            )
            store(h, total[:])

        with tc.manual_schedule():
            nc.scalar.copy(out=identity_bf16[:], in_=identity[:])
            nc.scalar.copy(
                out=exchange[:].rearrange("p (n c) -> p n c", c=2),
                in_=pairs_exchanged(identity[:]),
            )
            keep_tensor_busy(zeros[:].bitcast(BF16), 40)
            keep_tensor_busy(zeros[:], 512)
            transpose_weights(0)
            group_weights(0)
            transpose_positions()
            quantise_weights(0)
            keep_tensor_busy(zeros[:], 256)
            transpose_weights(1)
            group_weights(1)
            quantise_positions()
            exchange_sines()
            transpose_weights(2)
            group_weights(2)
            quantise_weights(1)
            multiply(0)
            flipped_tables = transpose_tables()
            copy_tables(flipped_tables)
            transpose_weights(3)
            group_weights(3)
            multiply(1)
            rotate(0, tables)
            add_and_store(0, nc.gpsimd)
            quantise_weights(2)
            transpose_weights(4)
            group_weights(4)
            multiply_t(2)
            multiply_t(3)
            fill(4, 2)
            rotate(1, tables)
            add_and_store(1, nc.gpsimd)
            quantise_weights(3)
            rotate(2, tables_t)
            multiply_t(4)
            multiply(5)
            copy_product(4)
            cosine_gpsimd(4, tables_t)
            fill(6, 1)
            add_t(2)
            store_t(2)
            rotate(3, tables_t)
            quantise_weights(4)
            add_t(3)
            store_t(3)
            multiply(6)
            multiply(7)
            rotate(5, tables)
            add_and_store(5, nc.gpsimd)
            rotate_one(4, tables_t, 1)
            add_t(4)
            store_t(4)
            rotate(6, tables)
            rotate(7, tables)
            add_and_store(6, nc.vector)
            add_and_store(7, nc.vector)
